import numpy as np
import ml_dtypes


def mxq(x, axis, fmt="e4m3"):
    dtype, down = {"e4m3": (ml_dtypes.float8_e4m3fn, 7), "e5m2": (ml_dtypes.float8_e5m2, 14)}[fmt]
    v = np.moveaxis(np.asarray(x, np.float32).astype(ml_dtypes.bfloat16).astype(np.float64), axis, -1)
    blocks = v.reshape(v.shape[:-1] + (-1, 32))
    amax = np.abs(blocks).max(-1, keepdims=True)
    byte = np.maximum(np.where(amax > 0, np.frexp(amax)[1] - 1 + 127, 0) - down, 1)
    scale = np.exp2(byte - 127.0)
    codes = (blocks / scale).astype(np.float32).astype(dtype).astype(np.float64)
    return np.moveaxis((codes * scale).reshape(v.shape), -1, axis)


WIDE = False


def mx_kscale(k):
    if not WIDE:
        return np.ones(k)
    levels = np.array([10, -10, 5, -5, 0])
    a = np.random.permutation(np.resize(levels, k // 512 * 4)).reshape(k // 512, 4)
    idx = np.arange(k)
    return np.exp2(a[idx // 512, idx % 128 // 32])


BF16 = ml_dtypes.bfloat16


def bf(x):
    return np.asarray(x, np.float32).astype(BF16)


def f64(x):
    return np.asarray(x).astype(np.float64)


B, N, D, F, C, L = 8192, 512, 1024, 1024, 128, 28
EPS = 1e-12
P = 3


def unit_rows(m, k):
    x = np.random.standard_normal((m, k))
    return x / np.sqrt(np.sum(x * x, axis=1, keepdims=True))


def setup_inputs():
    s = mx_kscale(F)
    return {"f_unit": bf(unit_rows(B, F) * s),
            "exf_unit": bf(unit_rows(N, F) / s),
            "ex_class_reps": bf((np.random.uniform(size=(N, C)) * 2.0 - 1.0) * 0.15 * np.sqrt(N)),
            "class_reps": bf((np.random.uniform(size=(L, C)) * 2.0 - 1.0) * 0.4)}


def reference(f_unit, exf_unit, ex_class_reps, class_reps):
    s = mxq(f64(f_unit), 1, "e4m3") @ mxq(f64(exf_unit), 1, "e4m3").T
    a = np.sign(s) * np.abs(s) ** P
    a = a / np.maximum(np.sum(np.abs(a), axis=1, keepdims=True), EPS)
    echo = mxq(a, 1, "e4m3") @ mxq(f64(ex_class_reps), 0, "e4m3")
    diff = echo[:, None, :] - f64(class_reps)[None, :, :]
    return -np.sqrt(np.sum(diff * diff, axis=-1))

@@ -1,0 +1,317 @@
+import concourse.mybir as mybir
+from concourse.masks import make_identity
+
+F32 = mybir.dt.float32
+BF16 = mybir.dt.bfloat16
+U32 = mybir.dt.uint32
+U8 = mybir.dt.uint8
+FP8X4 = mybir.dt.float8_e4m3fn_x4
+ACT = mybir.ActivationFunctionType
+ALU = mybir.AluOpType
+
+P = 128
+PACK = 4
+K_PASS = P * PACK
+HALVES = 2
+
+PROBES = 8192
+FEATURES = 1024
+EXEMPLARS = 512
+CLASS_DIM = 128
+CLASSES = 28
+CLASSES_PAD = 32
+EPS = 1e-12
+
+PASSES = FEATURES // K_PASS
+TILES = PROBES // P
+STEP_TILES = 2
+STEPS = TILES // STEP_TILES
+LOAD_TILES = 4
+LOAD_STEPS = LOAD_TILES // STEP_TILES
+LOADS = TILES // LOAD_TILES
+LOADS_AHEAD = 2
+STORE_TILES = 8
+STORE_STEPS = STORE_TILES // STEP_TILES
+
+FLOPS = 2 * PROBES * EXEMPLARS * (FEATURES + CLASS_DIM) + 3 * PROBES * CLASSES * CLASS_DIM
+
+
+def tile_minerva_old_pb_t_kernel(tc, f_unit, exf_unit, ex_class_reps, class_reps, out):
+    nc = tc.nc
+
+    f_view = f_unit.rearrange("(p t) k -> p t k", t=TILES)
+    out_view = out.rearrange("(p t) l -> p t l", t=TILES)
+
+    with tc.tile_pool(name="const", bufs=1) as const, \
+            tc.tile_pool(name="f_in", bufs=LOADS_AHEAD + 1) as f_in, \
+            tc.tile_pool(name="pair", bufs=2) as pair, \
+            tc.tile_pool(name="work", bufs=4) as work, \
+            tc.psum_pool(name="psum_ft", bufs=2) as psum_ft, \
+            tc.psum_pool(name="psum_s", bufs=3) as psum_s, \
+            tc.psum_pool(name="psum_at", bufs=1) as psum_at, \
+            tc.psum_pool(name="psum_echo", bufs=1) as psum_echo, \
+            tc.psum_pool(name="psum_d2", bufs=1) as psum_d2:
+
+        reps_raw = const.tile([P, PACK, CLASS_DIM], BF16)
+        nc.sync.dma_start(
+            out=reps_raw[:].rearrange("q (u e) c -> q u (e c)", u=HALVES),
+            in_=ex_class_reps.rearrange("(u q e) c -> q u (e c)", u=HALVES, q=P),
+        )
+        classes_bf = const.tile([P, CLASS_DIM], BF16)
+        nc.vector.memset(classes_bf[:], 0.0)
+        nc.sync.dma_start(out=classes_bf[0:CLASSES, :], in_=class_reps)
+        exf_raw = const.tile([P, EXEMPLARS // P, FEATURES], BF16)
+        nc.sync.dma_start(out=exf_raw[:], in_=exf_unit.rearrange("(i p) k -> p i k", p=P))
+
+        f_raw = {}
+
+        def load_f(load):
+            f_raw[load] = f_in.tile([P, LOAD_TILES, FEATURES], BF16, name="f_raw")
+            first = load * LOAD_TILES
+            nc.sync.dma_start(out=f_raw[load][:], in_=f_view[:, first:first + LOAD_TILES, :])
+
+        for load in range(LOADS_AHEAD):
+            load_f(load)
+
+        ident = const.tile([P, P], F32)
+        make_identity(nc, ident[:])
+        ones = const.tile([P, P], F32)
+        nc.vector.memset(ones[:], 1.0)
+        first_root = const.tile([P, 1], F32)
+        nc.scalar.activation(out=first_root[:], in_=ones[:, 0:1], func=ACT.Sqrt)
+
+        reps_grouped = const.tile([P, CLASS_DIM, PACK], BF16, align_bytes=64)
+        nc.vector.tensor_copy(out=reps_grouped[:], in_=reps_raw[:].rearrange("q t c -> q c t"))
+        reps_codes = const.tile([P, CLASS_DIM], U32, align_bytes=64)
+        reps_scales = const.tile([P, CLASS_DIM], U8, align_bytes=64)
+        nc.vector.quantize_mx(
+            out=reps_codes[:].bitcast(FP8X4),
+            scales=reps_scales[:],
+            in_=reps_grouped[:].rearrange("q c t -> q (c t)"),
+        )
+
+        classes_f32 = const.tile([P, CLASS_DIM], F32)
+        nc.vector.tensor_copy(out=classes_f32[:], in_=classes_bf[:])
+        classes_t = psum_at.tile([P, P], F32, tag="a_t")
+        nc.tensor.transpose(classes_t[:], classes_f32[:], ident[:])
+        minus_2r = const.tile([P, CLASSES_PAD], F32)
+        nc.vector.tensor_scalar(out=minus_2r[:], in0=classes_t[:, 0:CLASSES_PAD], scalar1=-2.0,
+                                scalar2=None, op0=ALU.mult)
+        r_squared = const.tile([P, CLASSES_PAD], F32)
+        nc.scalar.activation(out=r_squared[:], in_=classes_t[:, 0:CLASSES_PAD], func=ACT.Square)
+
+        exf_grouped = const.tile([P, PASSES, EXEMPLARS * PACK], BF16, align_bytes=64)
+        exf_words = exf_grouped[:].bitcast(F32).rearrange("p g (n u) -> p g n u", u=HALVES)
+        for i in range(EXEMPLARS // P):
+            exf_t = psum_ft.tile([P, PASSES, HALVES, P], F32, tag="f_t")
+            for w in range(PASSES * HALVES):
+                nc.tensor.transpose(exf_t[:, w // HALVES, w % HALVES, :],
+                                    exf_raw[:, i, :].bitcast(F32)[:, w * P:(w + 1) * P], ident[:])
+            nc.scalar.copy(out=exf_words[:, :, i * P:(i + 1) * P, :],
+                           in_=exf_t[:].rearrange("p g u n -> p g n u"))
+        exf_codes = const.tile([P, PASSES, EXEMPLARS], U32, align_bytes=64)
+        exf_scales = const.tile([P, PASSES, EXEMPLARS], U8, align_bytes=64)
+        for g in range(PASSES):
+            nc.vector.quantize_mx(out=exf_codes[:, g, :].bitcast(FP8X4), scales=exf_scales[:, g, :],
+                                  in_=exf_grouped[:, g, :])
+
+        f_t = {}
+        f_grouped = {}
+        f_codes = {}
+        f_scales = {}
+        s = {}
+        squares = {}
+        cubes = {}
+        row_sum = {}
+        a = {}
+        a_t = {}
+        a_grouped = {}
+        a_codes = {}
+        a_scales = {}
+        echo_t = {}
+        echo = {}
+        echo_sq = {}
+        d2 = {}
+        clamped = {}
+        roots = {}
+
+        def transpose_f(step):
+            for j in range(STEP_TILES):
+                tile = step * STEP_TILES + j
+                words = f_raw[tile // LOAD_TILES][:, tile % LOAD_TILES, :].bitcast(F32)
+                f_t[step, j] = psum_ft.tile([P, PASSES, HALVES, P], F32, name="f_t")
+                for w in range(PASSES * HALVES):
+                    nc.tensor.transpose(f_t[step, j][:, w // HALVES, w % HALVES, :],
+                                        words[:, w * P:(w + 1) * P], ident[:])
+
+        def regroup_f(step):
+            f_grouped[step] = pair.tile([P, STEP_TILES, PASSES, P * PACK], BF16, name="f_grouped",
+                                        align_bytes=64)
+            for j in range(STEP_TILES):
+                nc.scalar.copy(
+                    out=f_grouped[step][:, j].bitcast(F32).rearrange("p g (b u) -> p g b u", u=HALVES),
+                    in_=f_t[step, j][:].rearrange("p g u b -> p g b u"),
+                )
+
+        def quantise_f(step):
+            f_codes[step] = pair.tile([P, STEP_TILES, PASSES, P], U32, name="f_codes", align_bytes=64)
+            f_scales[step] = pair.tile([P, STEP_TILES, PASSES, P], U8, name="f_scales", align_bytes=64)
+            nc.vector.quantize_mx(
+                out=f_codes[step][:].rearrange("p j g b -> p (j g b)").bitcast(FP8X4),
+                scales=f_scales[step][:].rearrange("p j g b -> p (j g b)"),
+                in_=f_grouped[step][:].rearrange("p j g x -> p (j g x)"),
+            )
+
+        def similarities(step):
+            for j in range(STEP_TILES):
+                s[step, j] = psum_s.tile([P, EXEMPLARS], F32, name="s")
+                for g in range(PASSES):
+                    nc.tensor.matmul_mx(
+                        out=s[step, j][:],
+                        lhsT=f_codes[step][:, j, g, :].bitcast(FP8X4),
+                        lhsT_scale=f_scales[step][:, j, g, :],
+                        rhs=exf_codes[:, g, :].bitcast(FP8X4),
+                        rhs_scale=exf_scales[:, g, :],
+                        start=(g == 0),
+                        stop=(g == PASSES - 1),
+                    )
+
+        def square(step):
+            for j in range(STEP_TILES):
+                squares[step, j] = work.tile([P, EXEMPLARS], F32, name="squares")
+                nc.scalar.activation(out=squares[step, j][:], in_=s[step, j][:], func=ACT.Square)
+
+        def cube(step):
+            for j in range(STEP_TILES):
+                cubes[step, j] = work.tile([P, EXEMPLARS], F32, name="cubes")
+                nc.vector.tensor_tensor(out=cubes[step, j][:], in0=s[step, j][:],
+                                        in1=squares[step, j][:], op=ALU.mult)
+
+        def sum_rows(step):
+            row_sum[step] = pair.tile([P, STEP_TILES], F32, name="row_sum")
+            for j in range(STEP_TILES):
+                magnitudes = work.tile([P, EXEMPLARS], BF16, name="magnitudes")
+                nc.scalar.activation(out=magnitudes[:], in_=cubes[step, j][:], func=ACT.Abs,
+                                     accum_out=row_sum[step][:, j:j + 1])
+
+        def normalise(step):
+            inverse = pair.tile([P, STEP_TILES], F32, name="inverse")
+            nc.vector.tensor_scalar_max(out=inverse[:], in0=row_sum[step][:], scalar1=EPS)
+            nc.vector.reciprocal(out=inverse[:], in_=inverse[:])
+            a[step] = pair.tile([P, STEP_TILES, EXEMPLARS], BF16, name="a")
+            for j in range(STEP_TILES):
+                nc.vector.tensor_scalar(out=a[step][:, j, :], in0=cubes[step, j][:],
+                                        scalar1=inverse[:, j:j + 1], scalar2=None, op0=ALU.mult)
+
+        def transpose_a(step):
+            a_t[step] = psum_at.tile([P, STEP_TILES, HALVES, P], F32, name="a_t")
+            for j in range(STEP_TILES):
+                words = a[step][:, j, :].bitcast(F32)
+                for u in range(HALVES):
+                    nc.tensor.transpose(a_t[step][:, j, u, :], words[:, u * P:(u + 1) * P], ident[:])
+
+        def regroup_a(step):
+            a_grouped[step] = pair.tile([P, STEP_TILES, P * PACK], BF16, name="a_grouped",
+                                        align_bytes=64)
+            nc.vector.tensor_copy(
+                out=a_grouped[step][:].bitcast(F32).rearrange("p j (b u) -> p j b u", u=HALVES),
+                in_=a_t[step][:].rearrange("p j u b -> p j b u"),
+            )
+
+        def quantise_a(step):
+            a_codes[step] = pair.tile([P, STEP_TILES * P], U32, name="a_codes", align_bytes=64)
+            a_scales[step] = pair.tile([P, STEP_TILES * P], U8, name="a_scales", align_bytes=64)
+            nc.vector.quantize_mx(out=a_codes[step][:].bitcast(FP8X4), scales=a_scales[step][:],
+                                  in_=a_grouped[step][:].rearrange("p j x -> p (j x)"))
+
+        def echoes(step):
+            echo_t[step] = psum_echo.tile([P, STEP_TILES * P], F32, name="echo_t")
+            nc.tensor.matmul_mx(
+                out=echo_t[step][:],
+                lhsT=reps_codes[:].bitcast(FP8X4),
+                lhsT_scale=reps_scales[:],
+                rhs=a_codes[step][:].bitcast(FP8X4),
+                rhs_scale=a_scales[step][:],
+                start=True,
+                stop=True,
+            )
+
+        def copy_echo(step):
+            echo[step] = pair.tile([P, STEP_TILES * P], F32, name="echo")
+            nc.vector.tensor_copy(out=echo[step][:], in_=echo_t[step][:])
+
+        def square_echo(step):
+            echo_sq[step] = pair.tile([P, STEP_TILES * P], F32, name="echo_sq")
+            nc.scalar.activation(out=echo_sq[step][:], in_=echo[step][:], func=ACT.Square)
+
+        def squared_distances(step):
+            group = step // STORE_STEPS
+            if step % STORE_STEPS == 0:
+                d2[group] = psum_d2.tile([P, STORE_TILES, CLASSES_PAD], F32, name="d2")
+            for j in range(STEP_TILES):
+                place = d2[group][:, (step % STORE_STEPS) * STEP_TILES + j, :]
+                probes = slice(j * P, (j + 1) * P)
+                nc.tensor.matmul(out=place, lhsT=echo_sq[step][:, probes], rhs=ones[:, 0:CLASSES_PAD],
+                                 start=True, stop=False)
+                nc.tensor.matmul(out=place, lhsT=echo[step][:, probes], rhs=minus_2r[:],
+                                 start=False, stop=False)
+                nc.tensor.matmul(out=place, lhsT=ones[:], rhs=r_squared[:], start=False, stop=True)
+
+        def clamp(group):
+            clamped[group] = pair.tile([P, STORE_TILES, CLASSES_PAD], F32, name="clamped")
+            nc.vector.tensor_scalar_max(out=clamped[group][:], in0=d2[group][:], scalar1=0.0)
+
+        def root(group):
+            roots[group] = pair.tile([P, STORE_TILES, CLASSES_PAD], F32, name="roots")
+            nc.scalar.activation(out=roots[group][:], in_=clamped[group][:], func=ACT.Sqrt)
+
+        def negate_and_store(group):
+            result = pair.tile([P, STORE_TILES, CLASSES], F32, name="result")
+            nc.vector.tensor_scalar(out=result[:], in0=roots[group][:, :, 0:CLASSES], scalar1=-1.0,
+                                    scalar2=None, op0=ALU.mult)
+            first = group * STORE_TILES
+            nc.sync.dma_start(out=out_view[:, first:first + STORE_TILES, :], in_=result[:])
+
+        def in_range(step):
+            return 0 <= step < STEPS
+
+        LAST_LAG = 9
+        with tc.manual_schedule():
+            for k in range(STEPS + LAST_LAG):
+                if k % LOAD_STEPS == 0 and k // LOAD_STEPS + LOADS_AHEAD < LOADS:
+                    load_f(k // LOAD_STEPS + LOADS_AHEAD)
+                group_done = in_range(k - 9) and (k - 9) % STORE_STEPS == STORE_STEPS - 1
+                if in_range(k):
+                    transpose_f(k)
+                if in_range(k - 4):
+                    transpose_a(k - 4)
+                if in_range(k - 1):
+                    quantise_f(k - 1)
+                if group_done:
+                    clamp((k - 9) // STORE_STEPS)
+                if in_range(k - 1):
+                    similarities(k - 1)
+                if in_range(k - 2):
+                    square(k - 2)
+                    cube(k - 2)
+                if in_range(k - 8):
+                    squared_distances(k - 8)
+                if in_range(k - 3):
+                    sum_rows(k - 3)
+                if in_range(k - 7):
+                    copy_echo(k - 7)
+                if in_range(k - 6):
+                    echoes(k - 6)
+                if in_range(k - 5):
+                    quantise_a(k - 5)
+                if in_range(k - 3):
+                    normalise(k - 3)
+                if in_range(k - 4):
+                    regroup_a(k - 4)
+                if in_range(k):
+                    regroup_f(k)
+                if in_range(k - 7):
+                    square_echo(k - 7)
+                if group_done:
+                    root((k - 9) // STORE_STEPS)
+                    negate_and_store((k - 9) // STORE_STEPS)

@@ -99,6 +99,10 @@ def tile_minerva_old_pb_t_kernel(tc, f_unit, exf_unit, ex_class_reps, class_reps
                                 scalar2=None, op0=ALU.mult)
         r_squared = const.tile([P, CLASSES_PAD], F32)
         nc.scalar.activation(out=r_squared[:], in_=classes_t[:, 0:CLASSES_PAD], func=ACT.Square)
+        norms_psum = psum_d2.tile([P, CLASSES_PAD], F32, tag="d2")
+        nc.tensor.matmul(out=norms_psum[:], lhsT=ones[:], rhs=r_squared[:], start=True, stop=True)
+        class_norms = const.tile([P, CLASSES_PAD], F32)
+        nc.vector.tensor_copy(out=class_norms[:], in_=norms_psum[:])
 
         exf_grouped = const.tile([P, PASSES, EXEMPLARS * PACK], BF16, align_bytes=64)
         exf_words = exf_grouped[:].bitcast(F32).rearrange("p g (n u) -> p g n u", u=HALVES)
@@ -254,12 +258,15 @@ def tile_minerva_old_pb_t_kernel(tc, f_unit, exf_unit, ex_class_reps, class_reps
                 nc.tensor.matmul(out=place, lhsT=echo_sq[step][:, probes], rhs=ones[:, 0:CLASSES_PAD],
                                  start=True, stop=False)
                 nc.tensor.matmul(out=place, lhsT=echo[step][:, probes], rhs=minus_2r[:],
-                                 start=False, stop=False)
-                nc.tensor.matmul(out=place, lhsT=ones[:], rhs=r_squared[:], start=False, stop=True)
+                                 start=False, stop=True)
 
         def clamp(group):
+            summed = pair.tile([P, STORE_TILES, CLASSES_PAD], F32, name="summed")
+            nc.vector.tensor_tensor(
+                out=summed[:], in0=d2[group][:],
+                in1=class_norms[:].unsqueeze(1).to_broadcast([P, STORE_TILES, CLASSES_PAD]), op=ALU.add)
             clamped[group] = pair.tile([P, STORE_TILES, CLASSES_PAD], F32, name="clamped")
-            nc.vector.tensor_scalar_max(out=clamped[group][:], in0=d2[group][:], scalar1=0.0)
+            nc.vector.tensor_scalar_max(out=clamped[group][:], in0=summed[:], scalar1=0.0)
 
         def root(group):
             roots[group] = pair.tile([P, STORE_TILES, CLASSES_PAD], F32, name="roots")

@@ -24,14 +24,16 @@ EPS = 1e-12
 
 PASSES = FEATURES // K_PASS
 TILES = PROBES // P
+EX_TILES = EXEMPLARS // P
 STEP_TILES = 2
 STEPS = TILES // STEP_TILES
-LOAD_TILES = 4
+LOAD_TILES = 2
 LOAD_STEPS = LOAD_TILES // STEP_TILES
 LOADS = TILES // LOAD_TILES
-LOADS_AHEAD = 2
+LOADS_AHEAD = 4
 STORE_TILES = 8
 STORE_STEPS = STORE_TILES // STEP_TILES
+PSUM_BANKS = 8
 
 FLOPS = 2 * PROBES * EXEMPLARS * (FEATURES + CLASS_DIM) + 3 * PROBES * CLASSES * CLASS_DIM
 
@@ -46,11 +48,7 @@ def tile_minerva_old_pb_t_kernel(tc, f_unit, exf_unit, ex_class_reps, class_reps
             tc.tile_pool(name="f_in", bufs=LOADS_AHEAD + 1) as f_in, \
             tc.tile_pool(name="pair", bufs=2) as pair, \
             tc.tile_pool(name="work", bufs=4) as work, \
-            tc.psum_pool(name="psum_ft", bufs=2) as psum_ft, \
-            tc.psum_pool(name="psum_s", bufs=3) as psum_s, \
-            tc.psum_pool(name="psum_at", bufs=1) as psum_at, \
-            tc.psum_pool(name="psum_echo", bufs=1) as psum_echo, \
-            tc.psum_pool(name="psum_d2", bufs=1) as psum_d2:
+            tc.psum_pool(name="psum", bufs=PSUM_BANKS) as psum:
 
         reps_raw = const.tile([P, PACK, CLASS_DIM], BF16)
         nc.sync.dma_start(
@@ -60,8 +58,10 @@ def tile_minerva_old_pb_t_kernel(tc, f_unit, exf_unit, ex_class_reps, class_reps
         classes_bf = const.tile([P, CLASS_DIM], BF16)
         nc.vector.memset(classes_bf[:], 0.0)
         nc.sync.dma_start(out=classes_bf[0:CLASSES, :], in_=class_reps)
-        exf_raw = const.tile([P, EXEMPLARS // P, FEATURES], BF16)
-        nc.sync.dma_start(out=exf_raw[:], in_=exf_unit.rearrange("(i p) k -> p i k", p=P))
+        exf_raw = const.tile([P, EX_TILES, FEATURES], BF16)
+        exf_view = exf_unit.rearrange("(i p) k -> p i k", p=P)
+        for i in range(0, EX_TILES, 2):
+            nc.sync.dma_start(out=exf_raw[:, i:i + 2, :], in_=exf_view[:, i:i + 2, :])
 
         f_raw = {}
 
@@ -92,27 +92,28 @@ def tile_minerva_old_pb_t_kernel(tc, f_unit, exf_unit, ex_class_reps, class_reps
 
         classes_f32 = const.tile([P, CLASS_DIM], F32)
         nc.vector.tensor_copy(out=classes_f32[:], in_=classes_bf[:])
-        classes_t = psum_at.tile([P, P], F32, tag="a_t")
+        classes_t = psum.tile([P, P], F32, tag="bank")
         nc.tensor.transpose(classes_t[:], classes_f32[:], ident[:])
         minus_2r = const.tile([P, CLASSES_PAD], F32)
         nc.vector.tensor_scalar(out=minus_2r[:], in0=classes_t[:, 0:CLASSES_PAD], scalar1=-2.0,
                                 scalar2=None, op0=ALU.mult)
         r_squared = const.tile([P, CLASSES_PAD], F32)
         nc.scalar.activation(out=r_squared[:], in_=classes_t[:, 0:CLASSES_PAD], func=ACT.Square)
-        norms_psum = psum_d2.tile([P, CLASSES_PAD], F32, tag="d2")
+        norms_psum = psum.tile([P, CLASSES_PAD], F32, tag="bank")
         nc.tensor.matmul(out=norms_psum[:], lhsT=ones[:], rhs=r_squared[:], start=True, stop=True)
         class_norms = const.tile([P, CLASSES_PAD], F32)
         nc.vector.tensor_copy(out=class_norms[:], in_=norms_psum[:])
 
         exf_grouped = const.tile([P, PASSES, EXEMPLARS * PACK], BF16, align_bytes=64)
         exf_words = exf_grouped[:].bitcast(F32).rearrange("p g (n u) -> p g n u", u=HALVES)
-        for i in range(EXEMPLARS // P):
-            exf_t = psum_ft.tile([P, PASSES, HALVES, P], F32, tag="f_t")
+        for i in range(EX_TILES):
+            exf_t = psum.tile([P, PASSES, HALVES, P], F32, tag="bank")
             for w in range(PASSES * HALVES):
                 nc.tensor.transpose(exf_t[:, w // HALVES, w % HALVES, :],
                                     exf_raw[:, i, :].bitcast(F32)[:, w * P:(w + 1) * P], ident[:])
-            nc.scalar.copy(out=exf_words[:, :, i * P:(i + 1) * P, :],
-                           in_=exf_t[:].rearrange("p g u n -> p g n u"))
+            copy_out = nc.scalar.copy if i % 2 == 0 else nc.vector.tensor_copy
+            copy_out(out=exf_words[:, :, i * P:(i + 1) * P, :],
+                     in_=exf_t[:].rearrange("p g u n -> p g n u"))
         exf_codes = const.tile([P, PASSES, EXEMPLARS], U32, align_bytes=64)
         exf_scales = const.tile([P, PASSES, EXEMPLARS], U8, align_bytes=64)
         for g in range(PASSES):
@@ -143,7 +144,7 @@ def tile_minerva_old_pb_t_kernel(tc, f_unit, exf_unit, ex_class_reps, class_reps
             for j in range(STEP_TILES):
                 tile = step * STEP_TILES + j
                 words = f_raw[tile // LOAD_TILES][:, tile % LOAD_TILES, :].bitcast(F32)
-                f_t[step, j] = psum_ft.tile([P, PASSES, HALVES, P], F32, name="f_t")
+                f_t[step, j] = psum.tile([P, PASSES, HALVES, P], F32, name="f_t", tag="bank")
                 for w in range(PASSES * HALVES):
                     nc.tensor.transpose(f_t[step, j][:, w // HALVES, w % HALVES, :],
                                         words[:, w * P:(w + 1) * P], ident[:])
@@ -168,7 +169,7 @@ def tile_minerva_old_pb_t_kernel(tc, f_unit, exf_unit, ex_class_reps, class_reps
 
         def similarities(step):
             for j in range(STEP_TILES):
-                s[step, j] = psum_s.tile([P, EXEMPLARS], F32, name="s")
+                s[step, j] = psum.tile([P, EXEMPLARS], F32, name="s", tag="bank")
                 for g in range(PASSES):
                     nc.tensor.matmul_mx(
                         out=s[step, j][:],
@@ -204,11 +205,12 @@ def tile_minerva_old_pb_t_kernel(tc, f_unit, exf_unit, ex_class_reps, class_reps
             nc.vector.reciprocal(out=inverse[:], in_=inverse[:])
             a[step] = pair.tile([P, STEP_TILES, EXEMPLARS], BF16, name="a")
             for j in range(STEP_TILES):
-                nc.vector.tensor_scalar(out=a[step][:, j, :], in0=cubes[step, j][:],
-                                        scalar1=inverse[:, j:j + 1], scalar2=None, op0=ALU.mult)
+                nc.gpsimd.tensor_scalar(out=a[step][:, j, :], in0=cubes[step, j][:],
+                                        scalar1=inverse[:, j:j + 1], scalar2=0.0,
+                                        op0=ALU.mult, op1=ALU.add)
 
         def transpose_a(step):
-            a_t[step] = psum_at.tile([P, STEP_TILES, HALVES, P], F32, name="a_t")
+            a_t[step] = psum.tile([P, STEP_TILES, HALVES, P], F32, name="a_t", tag="bank")
             for j in range(STEP_TILES):
                 words = a[step][:, j, :].bitcast(F32)
                 for u in range(HALVES):
@@ -229,7 +231,7 @@ def tile_minerva_old_pb_t_kernel(tc, f_unit, exf_unit, ex_class_reps, class_reps
                                   in_=a_grouped[step][:].rearrange("p j x -> p (j x)"))
 
         def echoes(step):
-            echo_t[step] = psum_echo.tile([P, STEP_TILES * P], F32, name="echo_t")
+            echo_t[step] = psum.tile([P, STEP_TILES * P], F32, name="echo_t", tag="bank")
             nc.tensor.matmul_mx(
                 out=echo_t[step][:],
                 lhsT=reps_codes[:].bitcast(FP8X4),
@@ -246,12 +248,13 @@ def tile_minerva_old_pb_t_kernel(tc, f_unit, exf_unit, ex_class_reps, class_reps
 
         def square_echo(step):
             echo_sq[step] = pair.tile([P, STEP_TILES * P], F32, name="echo_sq")
-            nc.scalar.activation(out=echo_sq[step][:], in_=echo[step][:], func=ACT.Square)
+            nc.gpsimd.tensor_tensor(out=echo_sq[step][:], in0=echo[step][:], in1=echo[step][:],
+                                    op=ALU.mult)
 
         def squared_distances(step):
             group = step // STORE_STEPS
             if step % STORE_STEPS == 0:
-                d2[group] = psum_d2.tile([P, STORE_TILES, CLASSES_PAD], F32, name="d2")
+                d2[group] = psum.tile([P, STORE_TILES, CLASSES_PAD], F32, name="d2", tag="bank")
             for j in range(STEP_TILES):
                 place = d2[group][:, (step % STORE_STEPS) * STEP_TILES + j, :]
                 probes = slice(j * P, (j + 1) * P)
@@ -287,38 +290,37 @@ def tile_minerva_old_pb_t_kernel(tc, f_unit, exf_unit, ex_class_reps, class_reps
             for k in range(STEPS + LAST_LAG):
                 if k % LOAD_STEPS == 0 and k // LOAD_STEPS + LOADS_AHEAD < LOADS:
                     load_f(k // LOAD_STEPS + LOADS_AHEAD)
-                group_done = in_range(k - 9) and (k - 9) % STORE_STEPS == STORE_STEPS - 1
                 if in_range(k):
                     transpose_f(k)
                 if in_range(k - 4):
                     transpose_a(k - 4)
                 if in_range(k - 1):
-                    quantise_f(k - 1)
-                if group_done:
-                    clamp((k - 9) // STORE_STEPS)
-                if in_range(k - 1):
                     similarities(k - 1)
+                if in_range(k - 7):
+                    squared_distances(k - 7)
+                if in_range(k - 3):
+                    sum_rows(k - 3)
+                    normalise(k - 3)
+                if in_range(k - 6):
+                    copy_echo(k - 6)
+                if in_range(k - 5):
+                    echoes(k - 5)
+                if in_range(k - 6):
+                    square_echo(k - 6)
+                if in_range(k - 8) and (k - 8) % STORE_STEPS == STORE_STEPS - 1:
+                    clamp((k - 8) // STORE_STEPS)
                 if in_range(k - 2):
                     square(k - 2)
                     cube(k - 2)
-                if in_range(k - 8):
-                    squared_distances(k - 8)
-                if in_range(k - 3):
-                    sum_rows(k - 3)
-                if in_range(k - 7):
-                    copy_echo(k - 7)
-                if in_range(k - 6):
-                    echoes(k - 6)
-                if in_range(k - 5):
-                    quantise_a(k - 5)
-                if in_range(k - 3):
-                    normalise(k - 3)
                 if in_range(k - 4):
                     regroup_a(k - 4)
+                if in_range(k - 9) and (k - 9) % STORE_STEPS == STORE_STEPS - 1:
+                    negate_and_store((k - 9) // STORE_STEPS)
                 if in_range(k):
                     regroup_f(k)
-                if in_range(k - 7):
-                    square_echo(k - 7)
-                if group_done:
-                    root((k - 9) // STORE_STEPS)
-                    negate_and_store((k - 9) // STORE_STEPS)
+                if in_range(k - 8) and (k - 8) % STORE_STEPS == STORE_STEPS - 1:
+                    root((k - 8) // STORE_STEPS)
+                if in_range(k):
+                    quantise_f(k)
+                if in_range(k - 4):
+                    quantise_a(k - 4)

@@ -244,7 +244,7 @@ def tile_minerva_old_pb_t_kernel(tc, f_unit, exf_unit, ex_class_reps, class_reps
 
         def copy_echo(step):
             echo[step] = pair.tile([P, STEP_TILES * P], F32, name="echo")
-            nc.vector.tensor_copy(out=echo[step][:], in_=echo_t[step][:])
+            nc.scalar.copy(out=echo[step][:], in_=echo_t[step][:])
 
         def square_echo(step):
             echo_sq[step] = pair.tile([P, STEP_TILES * P], F32, name="echo_sq")

@@ -50,6 +50,19 @@ def tile_minerva_old_pb_t_kernel(tc, f_unit, exf_unit, ex_class_reps, class_reps
             tc.tile_pool(name="work", bufs=4) as work, \
             tc.psum_pool(name="psum", bufs=PSUM_BANKS) as psum:
 
+        f_raw = {}
+
+        def load_f(load):
+            f_raw[load] = f_in.tile([P, LOAD_TILES, FEATURES], BF16, name="f_raw")
+            first = load * LOAD_TILES
+            nc.sync.dma_start(out=f_raw[load][:], in_=f_view[:, first:first + LOAD_TILES, :])
+
+        load_f(0)
+        exf_raw = const.tile([P, EX_TILES, FEATURES], BF16)
+        exf_view = exf_unit.rearrange("(i p) k -> p i k", p=P)
+        for i in range(0, EX_TILES, 2):
+            nc.sync.dma_start(out=exf_raw[:, i:i + 2, :], in_=exf_view[:, i:i + 2, :])
+        load_f(1)
         reps_raw = const.tile([P, PACK, CLASS_DIM], BF16)
         nc.sync.dma_start(
             out=reps_raw[:].rearrange("q (u e) c -> q u (e c)", u=HALVES),
@@ -58,19 +71,7 @@ def tile_minerva_old_pb_t_kernel(tc, f_unit, exf_unit, ex_class_reps, class_reps
         classes_bf = const.tile([P, CLASS_DIM], BF16)
         nc.vector.memset(classes_bf[:], 0.0)
         nc.sync.dma_start(out=classes_bf[0:CLASSES, :], in_=class_reps)
-        exf_raw = const.tile([P, EX_TILES, FEATURES], BF16)
-        exf_view = exf_unit.rearrange("(i p) k -> p i k", p=P)
-        for i in range(0, EX_TILES, 2):
-            nc.sync.dma_start(out=exf_raw[:, i:i + 2, :], in_=exf_view[:, i:i + 2, :])
-
-        f_raw = {}
-
-        def load_f(load):
-            f_raw[load] = f_in.tile([P, LOAD_TILES, FEATURES], BF16, name="f_raw")
-            first = load * LOAD_TILES
-            nc.sync.dma_start(out=f_raw[load][:], in_=f_view[:, first:first + LOAD_TILES, :])
-
-        for load in range(LOADS_AHEAD):
+        for load in range(2, LOADS_AHEAD):
             load_f(load)
 
         ident = const.tile([P, P], F32)
@@ -81,44 +82,52 @@ def tile_minerva_old_pb_t_kernel(tc, f_unit, exf_unit, ex_class_reps, class_reps
         nc.scalar.activation(out=first_root[:], in_=ones[:, 0:1], func=ACT.Sqrt)
 
         reps_grouped = const.tile([P, CLASS_DIM, PACK], BF16, align_bytes=64)
-        nc.vector.tensor_copy(out=reps_grouped[:], in_=reps_raw[:].rearrange("q t c -> q c t"))
         reps_codes = const.tile([P, CLASS_DIM], U32, align_bytes=64)
         reps_scales = const.tile([P, CLASS_DIM], U8, align_bytes=64)
-        nc.vector.quantize_mx(
-            out=reps_codes[:].bitcast(FP8X4),
-            scales=reps_scales[:],
-            in_=reps_grouped[:].rearrange("q c t -> q (c t)"),
-        )
+
+        def set_up_reps():
+            nc.vector.tensor_copy(out=reps_grouped[:], in_=reps_raw[:].rearrange("q t c -> q c t"))
+            nc.vector.quantize_mx(
+                out=reps_codes[:].bitcast(FP8X4),
+                scales=reps_scales[:],
+                in_=reps_grouped[:].rearrange("q c t -> q (c t)"),
+            )
 
         classes_f32 = const.tile([P, CLASS_DIM], F32)
-        nc.vector.tensor_copy(out=classes_f32[:], in_=classes_bf[:])
-        classes_t = psum.tile([P, P], F32, tag="bank")
-        nc.tensor.transpose(classes_t[:], classes_f32[:], ident[:])
         minus_2r = const.tile([P, CLASSES_PAD], F32)
-        nc.vector.tensor_scalar(out=minus_2r[:], in0=classes_t[:, 0:CLASSES_PAD], scalar1=-2.0,
-                                scalar2=None, op0=ALU.mult)
         r_squared = const.tile([P, CLASSES_PAD], F32)
-        nc.scalar.activation(out=r_squared[:], in_=classes_t[:, 0:CLASSES_PAD], func=ACT.Square)
-        norms_psum = psum.tile([P, CLASSES_PAD], F32, tag="bank")
-        nc.tensor.matmul(out=norms_psum[:], lhsT=ones[:], rhs=r_squared[:], start=True, stop=True)
         class_norms = const.tile([P, CLASSES_PAD], F32)
-        nc.vector.tensor_copy(out=class_norms[:], in_=norms_psum[:])
+
+        def set_up_classes():
+            nc.vector.tensor_copy(out=classes_f32[:], in_=classes_bf[:])
+            classes_t = psum.tile([P, P], F32, tag="bank")
+            nc.tensor.transpose(classes_t[:], classes_f32[:], ident[:])
+            nc.vector.tensor_scalar(out=minus_2r[:], in0=classes_t[:, 0:CLASSES_PAD], scalar1=-2.0,
+                                    scalar2=None, op0=ALU.mult)
+            nc.scalar.activation(out=r_squared[:], in_=classes_t[:, 0:CLASSES_PAD], func=ACT.Square)
+
+        def set_up_class_norms():
+            norms_psum = psum.tile([P, CLASSES_PAD], F32, tag="bank")
+            nc.tensor.matmul(out=norms_psum[:], lhsT=ones[:], rhs=r_squared[:], start=True, stop=True)
+            nc.vector.tensor_copy(out=class_norms[:], in_=norms_psum[:])
 
         exf_grouped = const.tile([P, PASSES, EXEMPLARS * PACK], BF16, align_bytes=64)
-        exf_words = exf_grouped[:].bitcast(F32).rearrange("p g (n u) -> p g n u", u=HALVES)
-        for i in range(EX_TILES):
-            exf_t = psum.tile([P, PASSES, HALVES, P], F32, tag="bank")
-            for w in range(PASSES * HALVES):
-                nc.tensor.transpose(exf_t[:, w // HALVES, w % HALVES, :],
-                                    exf_raw[:, i, :].bitcast(F32)[:, w * P:(w + 1) * P], ident[:])
-            copy_out = nc.scalar.copy if i % 2 == 0 else nc.vector.tensor_copy
-            copy_out(out=exf_words[:, :, i * P:(i + 1) * P, :],
-                     in_=exf_t[:].rearrange("p g u n -> p g n u"))
         exf_codes = const.tile([P, PASSES, EXEMPLARS], U32, align_bytes=64)
         exf_scales = const.tile([P, PASSES, EXEMPLARS], U8, align_bytes=64)
-        for g in range(PASSES):
-            nc.vector.quantize_mx(out=exf_codes[:, g, :].bitcast(FP8X4), scales=exf_scales[:, g, :],
-                                  in_=exf_grouped[:, g, :])
+
+        def set_up_exf():
+            exf_words = exf_grouped[:].bitcast(F32).rearrange("p g (n u) -> p g n u", u=HALVES)
+            for i in range(EX_TILES):
+                exf_t = psum.tile([P, PASSES, HALVES, P], F32, tag="bank")
+                for w in range(PASSES * HALVES):
+                    nc.tensor.transpose(exf_t[:, w // HALVES, w % HALVES, :],
+                                        exf_raw[:, i, :].bitcast(F32)[:, w * P:(w + 1) * P], ident[:])
+                copy_out = nc.scalar.copy if i % 2 == 0 else nc.vector.tensor_copy
+                copy_out(out=exf_words[:, :, i * P:(i + 1) * P, :],
+                         in_=exf_t[:].rearrange("p g u n -> p g n u"))
+            for g in range(PASSES):
+                nc.vector.quantize_mx(out=exf_codes[:, g, :].bitcast(FP8X4), scales=exf_scales[:, g, :],
+                                      in_=exf_grouped[:, g, :])
 
         f_t = {}
         f_grouped = {}
@@ -324,3 +333,10 @@ def tile_minerva_old_pb_t_kernel(tc, f_unit, exf_unit, ex_class_reps, class_reps
                     quantise_f(k)
                 if in_range(k - 4):
                     quantise_a(k - 4)
+                if k == 0:
+                    set_up_exf()
+                if k == 1:
+                    set_up_reps()
+                    set_up_classes()
+                if k == 2:
+                    set_up_class_norms()

@@ -46,8 +46,8 @@ def tile_minerva_old_pb_t_kernel(tc, f_unit, exf_unit, ex_class_reps, class_reps
 
     with tc.tile_pool(name="const", bufs=1) as const, \
             tc.tile_pool(name="f_in", bufs=LOADS_AHEAD + 1) as f_in, \
-            tc.tile_pool(name="pair", bufs=2) as pair, \
-            tc.tile_pool(name="work", bufs=4) as work, \
+            tc.tile_pool(name="pair", bufs=4) as pair, \
+            tc.tile_pool(name="work", bufs=8) as work, \
             tc.psum_pool(name="psum", bufs=PSUM_BANKS) as psum:
 
         f_raw = {}
@@ -253,7 +253,7 @@ def tile_minerva_old_pb_t_kernel(tc, f_unit, exf_unit, ex_class_reps, class_reps
 
         def copy_echo(step):
             echo[step] = pair.tile([P, STEP_TILES * P], F32, name="echo")
-            nc.scalar.copy(out=echo[step][:], in_=echo_t[step][:])
+            nc.vector.tensor_copy(out=echo[step][:], in_=echo_t[step][:])
 
         def square_echo(step):
             echo_sq[step] = pair.tile([P, STEP_TILES * P], F32, name="echo_sq")

@@ -137,6 +137,8 @@ def tile_minerva_old_pb_t_kernel(tc, f_unit, exf_unit, ex_class_reps, class_reps
         squares = {}
         cubes = {}
         row_sum = {}
+        guarded = {}
+        inverse = {}
         a = {}
         a_t = {}
         a_grouped = {}
@@ -149,14 +151,13 @@ def tile_minerva_old_pb_t_kernel(tc, f_unit, exf_unit, ex_class_reps, class_reps
         clamped = {}
         roots = {}
 
-        def transpose_f(step):
-            for j in range(STEP_TILES):
-                tile = step * STEP_TILES + j
-                words = f_raw[tile // LOAD_TILES][:, tile % LOAD_TILES, :].bitcast(F32)
-                f_t[step, j] = psum.tile([P, PASSES, HALVES, P], F32, name="f_t", tag="bank")
-                for w in range(PASSES * HALVES):
-                    nc.tensor.transpose(f_t[step, j][:, w // HALVES, w % HALVES, :],
-                                        words[:, w * P:(w + 1) * P], ident[:])
+        def transpose_f(step, j):
+            tile = step * STEP_TILES + j
+            words = f_raw[tile // LOAD_TILES][:, tile % LOAD_TILES, :].bitcast(F32)
+            f_t[step, j] = psum.tile([P, PASSES, HALVES, P], F32, name="f_t", tag="bank")
+            for w in range(PASSES * HALVES):
+                nc.tensor.transpose(f_t[step, j][:, w // HALVES, w % HALVES, :],
+                                    words[:, w * P:(w + 1) * P], ident[:])
 
         def regroup_f(step):
             f_grouped[step] = pair.tile([P, STEP_TILES, PASSES, P * PACK], BF16, name="f_grouped",
@@ -176,19 +177,18 @@ def tile_minerva_old_pb_t_kernel(tc, f_unit, exf_unit, ex_class_reps, class_reps
                 in_=f_grouped[step][:].rearrange("p j g x -> p (j g x)"),
             )
 
-        def similarities(step):
-            for j in range(STEP_TILES):
-                s[step, j] = psum.tile([P, EXEMPLARS], F32, name="s", tag="bank")
-                for g in range(PASSES):
-                    nc.tensor.matmul_mx(
-                        out=s[step, j][:],
-                        lhsT=f_codes[step][:, j, g, :].bitcast(FP8X4),
-                        lhsT_scale=f_scales[step][:, j, g, :],
-                        rhs=exf_codes[:, g, :].bitcast(FP8X4),
-                        rhs_scale=exf_scales[:, g, :],
-                        start=(g == 0),
-                        stop=(g == PASSES - 1),
-                    )
+        def similarities(step, j):
+            s[step, j] = psum.tile([P, EXEMPLARS], F32, name="s", tag="bank")
+            for g in range(PASSES):
+                nc.tensor.matmul_mx(
+                    out=s[step, j][:],
+                    lhsT=f_codes[step][:, j, g, :].bitcast(FP8X4),
+                    lhsT_scale=f_scales[step][:, j, g, :],
+                    rhs=exf_codes[:, g, :].bitcast(FP8X4),
+                    rhs_scale=exf_scales[:, g, :],
+                    start=(g == 0),
+                    stop=(g == PASSES - 1),
+                )
 
         def square(step):
             for j in range(STEP_TILES):
@@ -208,14 +208,19 @@ def tile_minerva_old_pb_t_kernel(tc, f_unit, exf_unit, ex_class_reps, class_reps
                 nc.scalar.activation(out=magnitudes[:], in_=cubes[step, j][:], func=ACT.Abs,
                                      accum_out=row_sum[step][:, j:j + 1])
 
-        def normalise(step):
-            inverse = pair.tile([P, STEP_TILES], F32, name="inverse")
-            nc.vector.tensor_scalar_max(out=inverse[:], in0=row_sum[step][:], scalar1=EPS)
-            nc.vector.reciprocal(out=inverse[:], in_=inverse[:])
+        def guard(step):
+            guarded[step] = pair.tile([P, STEP_TILES], F32, name="guarded")
+            nc.vector.tensor_scalar_max(out=guarded[step][:], in0=row_sum[step][:], scalar1=EPS)
+
+        def invert(step):
+            inverse[step] = pair.tile([P, STEP_TILES], F32, name="inverse")
+            nc.vector.reciprocal(out=inverse[step][:], in_=guarded[step][:])
+
+        def scale(step):
             a[step] = pair.tile([P, STEP_TILES, EXEMPLARS], BF16, name="a")
             for j in range(STEP_TILES):
                 nc.gpsimd.tensor_scalar(out=a[step][:, j, :], in0=cubes[step, j][:],
-                                        scalar1=inverse[:, j:j + 1], scalar2=0.0,
+                                        scalar1=inverse[step][:, j:j + 1], scalar2=0.0,
                                         op0=ALU.mult, op1=ALU.add)
 
         def transpose_a(step):
@@ -294,45 +299,55 @@ def tile_minerva_old_pb_t_kernel(tc, f_unit, exf_unit, ex_class_reps, class_reps
         def in_range(step):
             return 0 <= step < STEPS
 
-        LAST_LAG = 9
+        def ends_group(step):
+            return in_range(step) and step % STORE_STEPS == STORE_STEPS - 1
+
+        LAST_LAG = 12
         with tc.manual_schedule():
             for k in range(STEPS + LAST_LAG):
                 if k % LOAD_STEPS == 0 and k // LOAD_STEPS + LOADS_AHEAD < LOADS:
                     load_f(k // LOAD_STEPS + LOADS_AHEAD)
                 if in_range(k):
-                    transpose_f(k)
-                if in_range(k - 4):
-                    transpose_a(k - 4)
-                if in_range(k - 1):
-                    similarities(k - 1)
-                if in_range(k - 7):
-                    squared_distances(k - 7)
-                if in_range(k - 3):
-                    sum_rows(k - 3)
-                    normalise(k - 3)
+                    transpose_f(k, 0)
                 if in_range(k - 6):
-                    copy_echo(k - 6)
-                if in_range(k - 5):
-                    echoes(k - 5)
-                if in_range(k - 6):
-                    square_echo(k - 6)
-                if in_range(k - 8) and (k - 8) % STORE_STEPS == STORE_STEPS - 1:
-                    clamp((k - 8) // STORE_STEPS)
+                    transpose_a(k - 6)
+                if in_range(k):
+                    transpose_f(k, 1)
                 if in_range(k - 2):
-                    square(k - 2)
-                    cube(k - 2)
+                    similarities(k - 2, 0)
                 if in_range(k - 4):
-                    regroup_a(k - 4)
-                if in_range(k - 9) and (k - 9) % STORE_STEPS == STORE_STEPS - 1:
-                    negate_and_store((k - 9) // STORE_STEPS)
+                    sum_rows(k - 4)
+                if in_range(k - 7):
+                    regroup_a(k - 7)
+                if ends_group(k - 11):
+                    clamp((k - 11) // STORE_STEPS)
+                if in_range(k - 5):
+                    invert(k - 5)
+                    scale(k - 5)
+                if in_range(k - 7):
+                    quantise_a(k - 7)
+                if in_range(k - 4):
+                    guard(k - 4)
+                if in_range(k - 3):
+                    square(k - 3)
+                    cube(k - 3)
+                if in_range(k - 10):
+                    squared_distances(k - 10)
+                if in_range(k - 7):
+                    echoes(k - 7)
+                if in_range(k - 8):
+                    copy_echo(k - 8)
+                    square_echo(k - 8)
                 if in_range(k):
                     regroup_f(k)
-                if in_range(k - 8) and (k - 8) % STORE_STEPS == STORE_STEPS - 1:
-                    root((k - 8) // STORE_STEPS)
+                if ends_group(k - 12):
+                    negate_and_store((k - 12) // STORE_STEPS)
+                if ends_group(k - 11):
+                    root((k - 11) // STORE_STEPS)
+                if in_range(k - 2):
+                    similarities(k - 2, 1)
                 if in_range(k):
                     quantise_f(k)
-                if in_range(k - 4):
-                    quantise_a(k - 4)
                 if k == 0:
                     set_up_exf()
                 if k == 1:

@@ -159,11 +159,11 @@ def tile_minerva_old_pb_t_kernel(tc, f_unit, exf_unit, ex_class_reps, class_reps
                 nc.tensor.transpose(f_t[step, j][:, w // HALVES, w % HALVES, :],
                                     words[:, w * P:(w + 1) * P], ident[:])
 
-        def regroup_f(step):
+        def regroup_f(step, copies):
             f_grouped[step] = pair.tile([P, STEP_TILES, PASSES, P * PACK], BF16, name="f_grouped",
                                         align_bytes=64)
             for j in range(STEP_TILES):
-                nc.scalar.copy(
+                copies[j](
                     out=f_grouped[step][:, j].bitcast(F32).rearrange("p g (b u) -> p g b u", u=HALVES),
                     in_=f_t[step, j][:].rearrange("p g u b -> p g b u"),
                 )
@@ -256,14 +256,16 @@ def tile_minerva_old_pb_t_kernel(tc, f_unit, exf_unit, ex_class_reps, class_reps
                 stop=True,
             )
 
-        def copy_echo(step):
+        def copy_and_square_echo(step, draining):
             echo[step] = pair.tile([P, STEP_TILES * P], F32, name="echo")
-            nc.vector.tensor_copy(out=echo[step][:], in_=echo_t[step][:])
-
-        def square_echo(step):
             echo_sq[step] = pair.tile([P, STEP_TILES * P], F32, name="echo_sq")
-            nc.gpsimd.tensor_tensor(out=echo_sq[step][:], in0=echo[step][:], in1=echo[step][:],
-                                    op=ALU.mult)
+            if draining:
+                nc.scalar.copy(out=echo[step][:], in_=echo_t[step][:])
+                nc.scalar.activation(out=echo_sq[step][:], in_=echo_t[step][:], func=ACT.Square)
+            else:
+                nc.vector.tensor_copy(out=echo[step][:], in_=echo_t[step][:])
+                nc.gpsimd.tensor_tensor(out=echo_sq[step][:], in0=echo[step][:], in1=echo[step][:],
+                                        op=ALU.mult)
 
         def squared_distances(step):
             group = step // STORE_STEPS
@@ -303,6 +305,8 @@ def tile_minerva_old_pb_t_kernel(tc, f_unit, exf_unit, ex_class_reps, class_reps
             return in_range(step) and step % STORE_STEPS == STORE_STEPS - 1
 
         LAST_LAG = 12
+        SET_UP_ROUNDS = 3
+        FIRST_A_ROUND = 7
         with tc.manual_schedule():
             for k in range(STEPS + LAST_LAG):
                 if k % LOAD_STEPS == 0 and k // LOAD_STEPS + LOADS_AHEAD < LOADS:
@@ -336,10 +340,10 @@ def tile_minerva_old_pb_t_kernel(tc, f_unit, exf_unit, ex_class_reps, class_reps
                 if in_range(k - 7):
                     echoes(k - 7)
                 if in_range(k - 8):
-                    copy_echo(k - 8)
-                    square_echo(k - 8)
+                    copy_and_square_echo(k - 8, draining=k >= STEPS)
                 if in_range(k):
-                    regroup_f(k)
+                    vector_has_room = SET_UP_ROUNDS <= k < FIRST_A_ROUND
+                    regroup_f(k, (nc.scalar.copy, nc.vector.tensor_copy if vector_has_room else nc.scalar.copy))
                 if ends_group(k - 12):
                     negate_and_store((k - 12) // STORE_STEPS)
                 if ends_group(k - 11):

@@ -46,8 +46,8 @@ def tile_minerva_old_pb_t_kernel(tc, f_unit, exf_unit, ex_class_reps, class_reps
 
     with tc.tile_pool(name="const", bufs=1) as const, \
             tc.tile_pool(name="f_in", bufs=LOADS_AHEAD + 1) as f_in, \
-            tc.tile_pool(name="pair", bufs=4) as pair, \
-            tc.tile_pool(name="work", bufs=8) as work, \
+            tc.tile_pool(name="pair", bufs=6) as pair, \
+            tc.tile_pool(name="work", bufs=12) as work, \
             tc.psum_pool(name="psum", bufs=PSUM_BANKS) as psum:
 
         f_raw = {}
@@ -203,10 +203,11 @@ def tile_minerva_old_pb_t_kernel(tc, f_unit, exf_unit, ex_class_reps, class_reps
 
         def sum_rows(step):
             row_sum[step] = pair.tile([P, STEP_TILES], F32, name="row_sum")
-            for j in range(STEP_TILES):
-                magnitudes = work.tile([P, EXEMPLARS], BF16, name="magnitudes")
-                nc.scalar.activation(out=magnitudes[:], in_=cubes[step, j][:], func=ACT.Abs,
-                                     accum_out=row_sum[step][:, j:j + 1])
+            magnitudes = work.tile([P, EXEMPLARS], BF16, name="magnitudes")
+            nc.scalar.activation(out=magnitudes[:], in_=cubes[step, 0][:], func=ACT.Abs,
+                                 accum_out=row_sum[step][:, 0:1])
+            nc.vector.tensor_reduce(out=row_sum[step][:, 1:2], in_=cubes[step, 1][:],
+                                    axis=mybir.AxisListType.X, op=ALU.add, apply_absolute_value=True)
 
         def guard(step):
             guarded[step] = pair.tile([P, STEP_TILES], F32, name="guarded")
@@ -233,7 +234,7 @@ def tile_minerva_old_pb_t_kernel(tc, f_unit, exf_unit, ex_class_reps, class_reps
         def regroup_a(step):
             a_grouped[step] = pair.tile([P, STEP_TILES, P * PACK], BF16, name="a_grouped",
                                         align_bytes=64)
-            nc.vector.tensor_copy(
+            nc.scalar.copy(
                 out=a_grouped[step][:].bitcast(F32).rearrange("p j (b u) -> p j b u", u=HALVES),
                 in_=a_t[step][:].rearrange("p j u b -> p j b u"),
             )
@@ -304,54 +305,53 @@ def tile_minerva_old_pb_t_kernel(tc, f_unit, exf_unit, ex_class_reps, class_reps
         def ends_group(step):
             return in_range(step) and step % STORE_STEPS == STORE_STEPS - 1
 
-        LAST_LAG = 12
+        LAST_LAG = 15
         SET_UP_ROUNDS = 3
-        FIRST_A_ROUND = 7
+        FIRST_A_ROUND = 8
         with tc.manual_schedule():
             for k in range(STEPS + LAST_LAG):
                 if k % LOAD_STEPS == 0 and k // LOAD_STEPS + LOADS_AHEAD < LOADS:
                     load_f(k // LOAD_STEPS + LOADS_AHEAD)
                 if in_range(k):
                     transpose_f(k, 0)
-                if in_range(k - 6):
-                    transpose_a(k - 6)
-                if in_range(k):
                     transpose_f(k, 1)
-                if in_range(k - 2):
-                    similarities(k - 2, 0)
+                if in_range(k - 9):
+                    quantise_a(k - 9)
                 if in_range(k - 4):
-                    sum_rows(k - 4)
-                if in_range(k - 7):
-                    regroup_a(k - 7)
-                if ends_group(k - 11):
-                    clamp((k - 11) // STORE_STEPS)
-                if in_range(k - 5):
-                    invert(k - 5)
-                    scale(k - 5)
-                if in_range(k - 7):
-                    quantise_a(k - 7)
-                if in_range(k - 4):
-                    guard(k - 4)
-                if in_range(k - 3):
-                    square(k - 3)
-                    cube(k - 3)
-                if in_range(k - 10):
-                    squared_distances(k - 10)
-                if in_range(k - 7):
-                    echoes(k - 7)
+                    square(k - 4)
                 if in_range(k - 8):
-                    copy_and_square_echo(k - 8, draining=k >= STEPS)
+                    regroup_a(k - 8)
+                if in_range(k - 6):
+                    invert(k - 6)
+                    scale(k - 6)
+                if in_range(k - 5):
+                    sum_rows(k - 5)
+                if in_range(k - 4):
+                    cube(k - 4)
+                if in_range(k - 3):
+                    similarities(k - 3, 0)
+                    similarities(k - 3, 1)
+                if in_range(k - 12):
+                    squared_distances(k - 12)
+                if ends_group(k - 13):
+                    clamp((k - 13) // STORE_STEPS)
+                if in_range(k - 9):
+                    echoes(k - 9)
+                if in_range(k - 10):
+                    copy_and_square_echo(k - 10, draining=k >= STEPS)
+                if ends_group(k - 14):
+                    root((k - 14) // STORE_STEPS)
+                if ends_group(k - 15):
+                    negate_and_store((k - 15) // STORE_STEPS)
+                if in_range(k - 5):
+                    guard(k - 5)
                 if in_range(k):
                     vector_has_room = SET_UP_ROUNDS <= k < FIRST_A_ROUND
                     regroup_f(k, (nc.scalar.copy, nc.vector.tensor_copy if vector_has_room else nc.scalar.copy))
-                if ends_group(k - 12):
-                    negate_and_store((k - 12) // STORE_STEPS)
-                if ends_group(k - 11):
-                    root((k - 11) // STORE_STEPS)
-                if in_range(k - 2):
-                    similarities(k - 2, 1)
-                if in_range(k):
-                    quantise_f(k)
+                if in_range(k - 1):
+                    quantise_f(k - 1)
+                if in_range(k - 7):
+                    transpose_a(k - 7)
                 if k == 0:
                     set_up_exf()
                 if k == 1:

@@ -19,7 +19,6 @@ FEATURES = 1024
 EXEMPLARS = 512
 CLASS_DIM = 128
 CLASSES = 28
-CLASSES_PAD = 32
 EPS = 1e-12
 
 PASSES = FEATURES // K_PASS
@@ -94,20 +93,20 @@ def tile_minerva_old_pb_t_kernel(tc, f_unit, exf_unit, ex_class_reps, class_reps
             )
 
         classes_f32 = const.tile([P, CLASS_DIM], F32)
-        minus_2r = const.tile([P, CLASSES_PAD], F32)
-        r_squared = const.tile([P, CLASSES_PAD], F32)
-        class_norms = const.tile([P, CLASSES_PAD], F32)
+        minus_2r = const.tile([P, CLASSES], F32)
+        r_squared = const.tile([P, CLASSES], F32)
+        class_norms = const.tile([P, CLASSES], F32)
 
         def set_up_classes():
             nc.vector.tensor_copy(out=classes_f32[:], in_=classes_bf[:])
             classes_t = psum.tile([P, P], F32, tag="bank")
             nc.tensor.transpose(classes_t[:], classes_f32[:], ident[:])
-            nc.vector.tensor_scalar(out=minus_2r[:], in0=classes_t[:, 0:CLASSES_PAD], scalar1=-2.0,
+            nc.vector.tensor_scalar(out=minus_2r[:], in0=classes_t[:, 0:CLASSES], scalar1=-2.0,
                                     scalar2=None, op0=ALU.mult)
-            nc.scalar.activation(out=r_squared[:], in_=classes_t[:, 0:CLASSES_PAD], func=ACT.Square)
+            nc.scalar.activation(out=r_squared[:], in_=classes_t[:, 0:CLASSES], func=ACT.Square)
 
         def set_up_class_norms():
-            norms_psum = psum.tile([P, CLASSES_PAD], F32, tag="bank")
+            norms_psum = psum.tile([P, CLASSES], F32, tag="bank")
             nc.tensor.matmul(out=norms_psum[:], lhsT=ones[:], rhs=r_squared[:], start=True, stop=True)
             nc.vector.tensor_copy(out=class_norms[:], in_=norms_psum[:])
 
@@ -271,30 +270,30 @@ def tile_minerva_old_pb_t_kernel(tc, f_unit, exf_unit, ex_class_reps, class_reps
         def squared_distances(step):
             group = step // STORE_STEPS
             if step % STORE_STEPS == 0:
-                d2[group] = psum.tile([P, STORE_TILES, CLASSES_PAD], F32, name="d2", tag="bank")
+                d2[group] = psum.tile([P, STORE_TILES, CLASSES], F32, name="d2", tag="bank")
             for j in range(STEP_TILES):
                 place = d2[group][:, (step % STORE_STEPS) * STEP_TILES + j, :]
                 probes = slice(j * P, (j + 1) * P)
-                nc.tensor.matmul(out=place, lhsT=echo_sq[step][:, probes], rhs=ones[:, 0:CLASSES_PAD],
+                nc.tensor.matmul(out=place, lhsT=echo_sq[step][:, probes], rhs=ones[:, 0:CLASSES],
                                  start=True, stop=False)
                 nc.tensor.matmul(out=place, lhsT=echo[step][:, probes], rhs=minus_2r[:],
                                  start=False, stop=True)
 
         def clamp(group):
-            summed = pair.tile([P, STORE_TILES, CLASSES_PAD], F32, name="summed")
+            summed = pair.tile([P, STORE_TILES, CLASSES], F32, name="summed")
             nc.vector.tensor_tensor(
                 out=summed[:], in0=d2[group][:],
-                in1=class_norms[:].unsqueeze(1).to_broadcast([P, STORE_TILES, CLASSES_PAD]), op=ALU.add)
-            clamped[group] = pair.tile([P, STORE_TILES, CLASSES_PAD], F32, name="clamped")
+                in1=class_norms[:].unsqueeze(1).to_broadcast([P, STORE_TILES, CLASSES]), op=ALU.add)
+            clamped[group] = pair.tile([P, STORE_TILES, CLASSES], F32, name="clamped")
             nc.vector.tensor_scalar_max(out=clamped[group][:], in0=summed[:], scalar1=0.0)
 
         def root(group):
-            roots[group] = pair.tile([P, STORE_TILES, CLASSES_PAD], F32, name="roots")
+            roots[group] = pair.tile([P, STORE_TILES, CLASSES], F32, name="roots")
             nc.scalar.activation(out=roots[group][:], in_=clamped[group][:], func=ACT.Sqrt)
 
         def negate_and_store(group):
             result = pair.tile([P, STORE_TILES, CLASSES], F32, name="result")
-            nc.vector.tensor_scalar(out=result[:], in0=roots[group][:, :, 0:CLASSES], scalar1=-1.0,
+            nc.vector.tensor_scalar(out=result[:], in0=roots[group][:], scalar1=-1.0,
                                     scalar2=None, op0=ALU.mult)
             first = group * STORE_TILES
             nc.sync.dma_start(out=out_view[:, first:first + STORE_TILES, :], in_=result[:])
@@ -330,7 +329,6 @@ def tile_minerva_old_pb_t_kernel(tc, f_unit, exf_unit, ex_class_reps, class_reps
                     cube(k - 4)
                 if in_range(k - 3):
                     similarities(k - 3, 0)
-                    similarities(k - 3, 1)
                 if in_range(k - 12):
                     squared_distances(k - 12)
                 if ends_group(k - 13):
@@ -348,6 +346,8 @@ def tile_minerva_old_pb_t_kernel(tc, f_unit, exf_unit, ex_class_reps, class_reps
                 if in_range(k):
                     vector_has_room = SET_UP_ROUNDS <= k < FIRST_A_ROUND
                     regroup_f(k, (nc.scalar.copy, nc.vector.tensor_copy if vector_has_room else nc.scalar.copy))
+                if in_range(k - 3):
+                    similarities(k - 3, 1)
                 if in_range(k - 1):
                     quantise_f(k - 1)
                 if in_range(k - 7):

import concourse.mybir as mybir
from concourse.masks import make_identity

F32 = mybir.dt.float32
BF16 = mybir.dt.bfloat16
U32 = mybir.dt.uint32
U8 = mybir.dt.uint8
FP8X4 = mybir.dt.float8_e4m3fn_x4
ACT = mybir.ActivationFunctionType
ALU = mybir.AluOpType

P = 128
PACK = 4
K_PASS = P * PACK
HALVES = 2

PROBES = 8192
FEATURES = 1024
EXEMPLARS = 512
CLASS_DIM = 128
CLASSES = 28
EPS = 1e-12

PASSES = FEATURES // K_PASS
TILES = PROBES // P
EX_TILES = EXEMPLARS // P
STEP_TILES = 2
STEPS = TILES // STEP_TILES
LOAD_TILES = 2
LOAD_STEPS = LOAD_TILES // STEP_TILES
LOADS = TILES // LOAD_TILES
LOADS_AHEAD = 4
STORE_TILES = 8
STORE_STEPS = STORE_TILES // STEP_TILES
PSUM_BANKS = 8

FLOPS = 2 * PROBES * EXEMPLARS * (FEATURES + CLASS_DIM) + 3 * PROBES * CLASSES * CLASS_DIM


def tile_minerva_old_pb_t_kernel(tc, f_unit, exf_unit, ex_class_reps, class_reps, out):
    nc = tc.nc

    f_view = f_unit.rearrange("(p t) k -> p t k", t=TILES)
    out_view = out.rearrange("(p t) l -> p t l", t=TILES)

    with tc.tile_pool(name="const", bufs=1) as const, \
            tc.tile_pool(name="f_in", bufs=LOADS_AHEAD + 1) as f_in, \
            tc.tile_pool(name="pair", bufs=6) as pair, \
            tc.tile_pool(name="work", bufs=12) as work, \
            tc.psum_pool(name="psum", bufs=PSUM_BANKS) as psum:

        f_raw = {}

        def load_f(load):
            f_raw[load] = f_in.tile([P, LOAD_TILES, FEATURES], BF16, name="f_raw")
            first = load * LOAD_TILES
            nc.sync.dma_start(out=f_raw[load][:], in_=f_view[:, first:first + LOAD_TILES, :])

        load_f(0)
        exf_raw = const.tile([P, EX_TILES, FEATURES], BF16)
        exf_view = exf_unit.rearrange("(i p) k -> p i k", p=P)
        for i in range(0, EX_TILES, 2):
            nc.sync.dma_start(out=exf_raw[:, i:i + 2, :], in_=exf_view[:, i:i + 2, :])
        load_f(1)
        reps_raw = const.tile([P, PACK, CLASS_DIM], BF16)
        nc.sync.dma_start(
            out=reps_raw[:].rearrange("q (u e) c -> q u (e c)", u=HALVES),
            in_=ex_class_reps.rearrange("(u q e) c -> q u (e c)", u=HALVES, q=P),
        )
        classes_bf = const.tile([P, CLASS_DIM], BF16)
        nc.vector.memset(classes_bf[:], 0.0)
        nc.sync.dma_start(out=classes_bf[0:CLASSES, :], in_=class_reps)
        for load in range(2, LOADS_AHEAD):
            load_f(load)

        ident = const.tile([P, P], F32)
        make_identity(nc, ident[:])
        ones = const.tile([P, P], F32)
        nc.vector.memset(ones[:], 1.0)
        first_root = const.tile([P, 1], F32)
        nc.scalar.activation(out=first_root[:], in_=ones[:, 0:1], func=ACT.Sqrt)

        reps_grouped = const.tile([P, CLASS_DIM, PACK], BF16, align_bytes=64)
        reps_codes = const.tile([P, CLASS_DIM], U32, align_bytes=64)
        reps_scales = const.tile([P, CLASS_DIM], U8, align_bytes=64)

        def set_up_reps():
            nc.vector.tensor_copy(out=reps_grouped[:], in_=reps_raw[:].rearrange("q t c -> q c t"))
            nc.vector.quantize_mx(
                out=reps_codes[:].bitcast(FP8X4),
                scales=reps_scales[:],
                in_=reps_grouped[:].rearrange("q c t -> q (c t)"),
            )

        classes_f32 = const.tile([P, CLASS_DIM], F32)
        minus_2r = const.tile([P, CLASSES], F32)
        r_squared = const.tile([P, CLASSES], F32)
        class_norms = const.tile([P, CLASSES], F32)

        def set_up_classes():
            nc.vector.tensor_copy(out=classes_f32[:], in_=classes_bf[:])
            classes_t = psum.tile([P, P], F32, tag="bank")
            nc.tensor.transpose(classes_t[:], classes_f32[:], ident[:])
            nc.vector.tensor_scalar(out=minus_2r[:], in0=classes_t[:, 0:CLASSES], scalar1=-2.0,
                                    scalar2=None, op0=ALU.mult)
            nc.scalar.activation(out=r_squared[:], in_=classes_t[:, 0:CLASSES], func=ACT.Square)

        def set_up_class_norms():
            norms_psum = psum.tile([P, CLASSES], F32, tag="bank")
            nc.tensor.matmul(out=norms_psum[:], lhsT=ones[:], rhs=r_squared[:], start=True, stop=True)
            nc.vector.tensor_copy(out=class_norms[:], in_=norms_psum[:])

        exf_grouped = const.tile([P, PASSES, EXEMPLARS * PACK], BF16, align_bytes=64)
        exf_codes = const.tile([P, PASSES, EXEMPLARS], U32, align_bytes=64)
        exf_scales = const.tile([P, PASSES, EXEMPLARS], U8, align_bytes=64)

        def set_up_exf():
            exf_words = exf_grouped[:].bitcast(F32).rearrange("p g (n u) -> p g n u", u=HALVES)
            for i in range(EX_TILES):
                exf_t = psum.tile([P, PASSES, HALVES, P], F32, tag="bank")
                for w in range(PASSES * HALVES):
                    nc.tensor.transpose(exf_t[:, w // HALVES, w % HALVES, :],
                                        exf_raw[:, i, :].bitcast(F32)[:, w * P:(w + 1) * P], ident[:])
                copy_out = nc.scalar.copy if i % 2 == 0 else nc.vector.tensor_copy
                copy_out(out=exf_words[:, :, i * P:(i + 1) * P, :],
                         in_=exf_t[:].rearrange("p g u n -> p g n u"))
            for g in range(PASSES):
                nc.vector.quantize_mx(out=exf_codes[:, g, :].bitcast(FP8X4), scales=exf_scales[:, g, :],
                                      in_=exf_grouped[:, g, :])

        f_t = {}
        f_grouped = {}
        f_codes = {}
        f_scales = {}
        s = {}
        squares = {}
        cubes = {}
        row_sum = {}
        guarded = {}
        inverse = {}
        a = {}
        a_t = {}
        a_grouped = {}
        a_codes = {}
        a_scales = {}
        echo_t = {}
        echo = {}
        echo_sq = {}
        d2 = {}
        clamped = {}
        roots = {}

        def transpose_f(step, j):
            tile = step * STEP_TILES + j
            words = f_raw[tile // LOAD_TILES][:, tile % LOAD_TILES, :].bitcast(F32)
            f_t[step, j] = psum.tile([P, PASSES, HALVES, P], F32, name="f_t", tag="bank")
            for w in range(PASSES * HALVES):
                nc.tensor.transpose(f_t[step, j][:, w // HALVES, w % HALVES, :],
                                    words[:, w * P:(w + 1) * P], ident[:])

        def regroup_f(step, copies):
            f_grouped[step] = pair.tile([P, STEP_TILES, PASSES, P * PACK], BF16, name="f_grouped",
                                        align_bytes=64)
            for j in range(STEP_TILES):
                copies[j](
                    out=f_grouped[step][:, j].bitcast(F32).rearrange("p g (b u) -> p g b u", u=HALVES),
                    in_=f_t[step, j][:].rearrange("p g u b -> p g b u"),
                )

        def quantise_f(step):
            f_codes[step] = pair.tile([P, STEP_TILES, PASSES, P], U32, name="f_codes", align_bytes=64)
            f_scales[step] = pair.tile([P, STEP_TILES, PASSES, P], U8, name="f_scales", align_bytes=64)
            nc.vector.quantize_mx(
                out=f_codes[step][:].rearrange("p j g b -> p (j g b)").bitcast(FP8X4),
                scales=f_scales[step][:].rearrange("p j g b -> p (j g b)"),
                in_=f_grouped[step][:].rearrange("p j g x -> p (j g x)"),
            )

        def similarities(step, j):
            s[step, j] = psum.tile([P, EXEMPLARS], F32, name="s", tag="bank")
            for g in range(PASSES):
                nc.tensor.matmul_mx(
                    out=s[step, j][:],
                    lhsT=f_codes[step][:, j, g, :].bitcast(FP8X4),
                    lhsT_scale=f_scales[step][:, j, g, :],
                    rhs=exf_codes[:, g, :].bitcast(FP8X4),
                    rhs_scale=exf_scales[:, g, :],
                    start=(g == 0),
                    stop=(g == PASSES - 1),
                )

        def square(step):
            for j in range(STEP_TILES):
                squares[step, j] = work.tile([P, EXEMPLARS], F32, name="squares")
                nc.scalar.activation(out=squares[step, j][:], in_=s[step, j][:], func=ACT.Square)

        def cube(step):
            for j in range(STEP_TILES):
                cubes[step, j] = work.tile([P, EXEMPLARS], F32, name="cubes")
                nc.vector.tensor_tensor(out=cubes[step, j][:], in0=s[step, j][:],
                                        in1=squares[step, j][:], op=ALU.mult)

        def sum_rows(step):
            row_sum[step] = pair.tile([P, STEP_TILES], F32, name="row_sum")
            magnitudes = work.tile([P, EXEMPLARS], BF16, name="magnitudes")
            nc.scalar.activation(out=magnitudes[:], in_=cubes[step, 0][:], func=ACT.Abs,
                                 accum_out=row_sum[step][:, 0:1])
            nc.vector.tensor_reduce(out=row_sum[step][:, 1:2], in_=cubes[step, 1][:],
                                    axis=mybir.AxisListType.X, op=ALU.add, apply_absolute_value=True)

        def guard(step):
            guarded[step] = pair.tile([P, STEP_TILES], F32, name="guarded")
            nc.vector.tensor_scalar_max(out=guarded[step][:], in0=row_sum[step][:], scalar1=EPS)

        def invert(step):
            inverse[step] = pair.tile([P, STEP_TILES], F32, name="inverse")
            nc.vector.reciprocal(out=inverse[step][:], in_=guarded[step][:])

        def scale(step):
            a[step] = pair.tile([P, STEP_TILES, EXEMPLARS], BF16, name="a")
            for j in range(STEP_TILES):
                nc.gpsimd.tensor_scalar(out=a[step][:, j, :], in0=cubes[step, j][:],
                                        scalar1=inverse[step][:, j:j + 1], scalar2=0.0,
                                        op0=ALU.mult, op1=ALU.add)

        def transpose_a(step):
            a_t[step] = psum.tile([P, STEP_TILES, HALVES, P], F32, name="a_t", tag="bank")
            for j in range(STEP_TILES):
                words = a[step][:, j, :].bitcast(F32)
                for u in range(HALVES):
                    nc.tensor.transpose(a_t[step][:, j, u, :], words[:, u * P:(u + 1) * P], ident[:])

        def regroup_a(step):
            a_grouped[step] = pair.tile([P, STEP_TILES, P * PACK], BF16, name="a_grouped",
                                        align_bytes=64)
            nc.scalar.copy(
                out=a_grouped[step][:].bitcast(F32).rearrange("p j (b u) -> p j b u", u=HALVES),
                in_=a_t[step][:].rearrange("p j u b -> p j b u"),
            )

        def quantise_a(step):
            a_codes[step] = pair.tile([P, STEP_TILES * P], U32, name="a_codes", align_bytes=64)
            a_scales[step] = pair.tile([P, STEP_TILES * P], U8, name="a_scales", align_bytes=64)
            nc.vector.quantize_mx(out=a_codes[step][:].bitcast(FP8X4), scales=a_scales[step][:],
                                  in_=a_grouped[step][:].rearrange("p j x -> p (j x)"))

        def echoes(step):
            echo_t[step] = psum.tile([P, STEP_TILES * P], F32, name="echo_t", tag="bank")
            nc.tensor.matmul_mx(
                out=echo_t[step][:],
                lhsT=reps_codes[:].bitcast(FP8X4),
                lhsT_scale=reps_scales[:],
                rhs=a_codes[step][:].bitcast(FP8X4),
                rhs_scale=a_scales[step][:],
                start=True,
                stop=True,
            )

        def copy_and_square_echo(step, draining):
            echo[step] = pair.tile([P, STEP_TILES * P], F32, name="echo")
            echo_sq[step] = pair.tile([P, STEP_TILES * P], F32, name="echo_sq")
            if draining:
                nc.scalar.copy(out=echo[step][:], in_=echo_t[step][:])
                nc.scalar.activation(out=echo_sq[step][:], in_=echo_t[step][:], func=ACT.Square)
            else:
                nc.vector.tensor_copy(out=echo[step][:], in_=echo_t[step][:])
                nc.gpsimd.tensor_tensor(out=echo_sq[step][:], in0=echo[step][:], in1=echo[step][:],
                                        op=ALU.mult)

        def squared_distances(step):
            group = step // STORE_STEPS
            if step % STORE_STEPS == 0:
                d2[group] = psum.tile([P, STORE_TILES, CLASSES], F32, name="d2", tag="bank")
            for j in range(STEP_TILES):
                place = d2[group][:, (step % STORE_STEPS) * STEP_TILES + j, :]
                probes = slice(j * P, (j + 1) * P)
                nc.tensor.matmul(out=place, lhsT=echo_sq[step][:, probes], rhs=ones[:, 0:CLASSES],
                                 start=True, stop=False)
                nc.tensor.matmul(out=place, lhsT=echo[step][:, probes], rhs=minus_2r[:],
                                 start=False, stop=True)

        def clamp(group):
            summed = pair.tile([P, STORE_TILES, CLASSES], F32, name="summed")
            nc.vector.tensor_tensor(
                out=summed[:], in0=d2[group][:],
                in1=class_norms[:].unsqueeze(1).to_broadcast([P, STORE_TILES, CLASSES]), op=ALU.add)
            clamped[group] = pair.tile([P, STORE_TILES, CLASSES], F32, name="clamped")
            nc.vector.tensor_scalar_max(out=clamped[group][:], in0=summed[:], scalar1=0.0)

        def root(group):
            roots[group] = pair.tile([P, STORE_TILES, CLASSES], F32, name="roots")
            nc.scalar.activation(out=roots[group][:], in_=clamped[group][:], func=ACT.Sqrt)

        def negate_and_store(group):
            result = pair.tile([P, STORE_TILES, CLASSES], F32, name="result")
            nc.vector.tensor_scalar(out=result[:], in0=roots[group][:], scalar1=-1.0,
                                    scalar2=None, op0=ALU.mult)
            first = group * STORE_TILES
            nc.sync.dma_start(out=out_view[:, first:first + STORE_TILES, :], in_=result[:])

        def in_range(step):
            return 0 <= step < STEPS

        def ends_group(step):
            return in_range(step) and step % STORE_STEPS == STORE_STEPS - 1

        LAST_LAG = 15
        SET_UP_ROUNDS = 3
        FIRST_A_ROUND = 8
        with tc.manual_schedule():
            for k in range(STEPS + LAST_LAG):
                if k % LOAD_STEPS == 0 and k // LOAD_STEPS + LOADS_AHEAD < LOADS:
                    load_f(k // LOAD_STEPS + LOADS_AHEAD)
                if in_range(k):
                    transpose_f(k, 0)
                    transpose_f(k, 1)
                if in_range(k - 9):
                    quantise_a(k - 9)
                if in_range(k - 4):
                    square(k - 4)
                if in_range(k - 8):
                    regroup_a(k - 8)
                if in_range(k - 6):
                    invert(k - 6)
                    scale(k - 6)
                if in_range(k - 5):
                    sum_rows(k - 5)
                if in_range(k - 4):
                    cube(k - 4)
                if in_range(k - 3):
                    similarities(k - 3, 0)
                if in_range(k - 12):
                    squared_distances(k - 12)
                if ends_group(k - 13):
                    clamp((k - 13) // STORE_STEPS)
                if in_range(k - 9):
                    echoes(k - 9)
                if in_range(k - 10):
                    copy_and_square_echo(k - 10, draining=k >= STEPS)
                if ends_group(k - 14):
                    root((k - 14) // STORE_STEPS)
                if ends_group(k - 15):
                    negate_and_store((k - 15) // STORE_STEPS)
                if in_range(k - 5):
                    guard(k - 5)
                if in_range(k):
                    vector_has_room = SET_UP_ROUNDS <= k < FIRST_A_ROUND
                    regroup_f(k, (nc.scalar.copy, nc.vector.tensor_copy if vector_has_room else nc.scalar.copy))
                if in_range(k - 3):
                    similarities(k - 3, 1)
                if in_range(k - 1):
                    quantise_f(k - 1)
                if in_range(k - 7):
                    transpose_a(k - 7)
                if k == 0:
                    set_up_exf()
                if k == 1:
                    set_up_reps()
                    set_up_classes()
                if k == 2:
                    set_up_class_norms()
